import numpy as np
import ml_dtypes


def mxq(x, axis, fmt="e4m3"):
    dtype, down = {"e4m3": (ml_dtypes.float8_e4m3fn, 7), "e5m2": (ml_dtypes.float8_e5m2, 14)}[fmt]
    v = np.moveaxis(np.asarray(x, np.float32).astype(ml_dtypes.bfloat16).astype(np.float64), axis, -1)
    blocks = v.reshape(v.shape[:-1] + (-1, 32))
    amax = np.abs(blocks).max(-1, keepdims=True)
    byte = np.maximum(np.where(amax > 0, np.frexp(amax)[1] - 1 + 127, 0) - down, 1)
    scale = np.exp2(byte - 127.0)
    codes = (blocks / scale).astype(np.float32).astype(dtype).astype(np.float64)
    return np.moveaxis((codes * scale).reshape(v.shape), -1, axis)


WIDE = False


def mx_kscale(k):
    if not WIDE:
        return np.ones(k)
    levels = np.array([30, -30])
    if k % 512:
        return np.exp2(np.random.permutation(np.resize(levels, k // 32))).repeat(32)
    a = np.empty((k // 512, 16))
    for p in range(k // 512):
        a[p, :8] = np.random.permutation(np.resize(levels, 8))
        for g in range(8):
            far = levels[np.abs(levels - a[p, g]) >= 10]
            a[p, g + 8] = far[np.random.randint(len(far))]
    return np.exp2(a.ravel()).repeat(32)


BF16 = ml_dtypes.bfloat16


def bf(x):
    return np.asarray(x, np.float32).astype(BF16)


def f64(x):
    return np.asarray(x).astype(np.float64)


E2M1 = np.array([0.0, 0.5, 1.0, 1.5, 2.0, 3.0, 4.0, 6.0, -0.0, -0.5, -1.0, -1.5, -2.0, -3.0, -4.0, -6.0])


def pack_weight(w, fmt):
    k, n = w.shape
    w = f64(bf(w)).reshape(k // 32, 32, n)
    amax = np.abs(w).max(1)
    if fmt == "e4m3":
        byte = np.frexp(amax)[1] - 1 + 127 - 7
    else:
        mant, ex = np.frexp(amax / 6.0)
        byte = np.where(mant > 0.5, ex, ex - 1) + 127
    byte = np.clip(np.where(amax > 0, byte, 1), 1, 254)
    scaled = (w * np.exp2(127.0 - byte)[:, None, :]).reshape(k, n).astype(np.float32)
    by_word = np.ascontiguousarray(scaled.reshape(k // 512, 128, 4, n).transpose(0, 1, 3, 2))
    if fmt == "e4m3":
        words = by_word.astype(ml_dtypes.float8_e4m3fn).view(np.uint8)
    else:
        c = by_word.astype(ml_dtypes.float4_e2m1fn).view(np.uint8) & 0xF
        words = c[..., 0::2] | (c[..., 1::2] << 4)
    return np.ascontiguousarray(words), np.ascontiguousarray(byte.astype(np.uint8).reshape(k // 512, 16, n))


def unpack_weight(words, scales, fmt):
    g, p, n, _ = words.shape
    if fmt == "e4m3":
        vals = np.ascontiguousarray(words).view(ml_dtypes.float8_e4m3fn).astype(np.float64)
    else:
        nib = np.empty((g, p, n, 4), np.uint8)
        nib[..., 0::2] = words & 0xF
        nib[..., 1::2] = words >> 4
        vals = E2M1[nib]
    vals = vals * np.repeat(np.exp2(scales.astype(np.float64) - 127.0), 8, axis=1)[..., None]
    return vals.transpose(0, 1, 3, 2).reshape(g * 512, n)

def pack4(w):
    words, scales = pack_weight(w, "e2m1")
    return words.reshape(words.shape[0], 128, -1), scales


def unpack4(words, scales):
    return unpack_weight(words.reshape(words.shape[0], 128, -1, 2), scales, "e2m1")


B, S, D, NH, NKV, HD = 1, 512, 2048, 16, 4, 128
ROPE_THETA = 10000.0


def rope_tables():
    freqs = 1.0 / (ROPE_THETA ** (f64(np.arange(0, HD, 2)) / HD))
    ang = np.outer(f64(np.arange(S)), freqs)
    return np.cos(ang), np.sin(ang)


def rope(x, cos, sin):
    xr = x.reshape(*x.shape[:-1], HD // 2, 2)
    re, im = xr[..., 0], xr[..., 1]
    c = cos[None, :, None, :]
    s = sin[None, :, None, :]
    return np.stack((re * c - im * s, re * s + im * c), axis=-1).reshape(x.shape)


def setup_inputs():
    s = mx_kscale(D)
    hidden_states = bf(np.random.standard_normal((B, S, D)) * s)
    wq_words, wq_scales = pack4(np.random.standard_normal((D, NH * HD)) / np.sqrt(D) / s[:, None])
    wk_words, wk_scales = pack4(np.random.standard_normal((D, NKV * HD)) / np.sqrt(D) / s[:, None])
    wv_words, wv_scales = pack4(np.random.standard_normal((D, NKV * HD)) * 2.0 / np.sqrt(D) / s[:, None])
    return {"hidden_states": hidden_states,
            "wq_words": wq_words, "wq_scales": wq_scales,
            "wk_words": wk_words, "wk_scales": wk_scales,
            "wv_words": wv_words, "wv_scales": wv_scales}


def reference(hidden_states, wq_words, wq_scales, wk_words, wk_scales, wv_words, wv_scales):
    xq = mxq(f64(hidden_states), 2, "e5m2")
    q = (xq @ unpack4(wq_words, wq_scales)).reshape(B, S, NH, HD)
    k = (xq @ unpack4(wk_words, wk_scales)).reshape(B, S, NKV, HD)
    v = (xq @ unpack4(wv_words, wv_scales)).reshape(B, S, NKV, HD)
    cos, sin = rope_tables()
    return rope(q, cos, sin), rope(k, cos, sin), v

@@ -1,0 +1,231 @@
+from contextlib import ExitStack
+
+import concourse.mybir as mybir
+from concourse.masks import make_identity
+
+FLOPS = 2 * 512 * 2048 * 3072
+
+F32 = mybir.dt.float32
+BF16 = mybir.dt.bfloat16
+I32 = mybir.dt.int32
+U32 = mybir.dt.uint32
+U8 = mybir.dt.uint8
+E5M2X4 = mybir.dt.float8_e5m2_x4
+E2M1X4 = mybir.dt.float4_e2m1fn_x4
+ALU = mybir.AluOpType
+ACT = mybir.ActivationFunctionType
+
+P = 128
+TOKEN_TILES = 4
+PASSES = 4
+N_TILE = 512
+HEADS_PER_TILE = 4
+PAIRS = 64
+ROPE_THETA = 10000.0
+TWO_PI = 6.283185307179586
+
+
+def tile_rptattention_pa_kernel(
+    tc, hidden_states, wq_words, wq_scales, wk_words, wk_scales, wv_words, wv_scales, out_0, out_1, out_2
+):
+    nc = tc.nc
+    x = hidden_states.flatten_outer_dims()
+    q_out = out_0.rearrange("b s h d -> (b s) (h d)")
+    k_out = out_1.rearrange("b s h d -> (b s) (h d)")
+    v_out = out_2.rearrange("b s h d -> (b s) (h d)")
+
+    with ExitStack() as ctx:
+        const = ctx.enter_context(tc.tile_pool(name="const", bufs=1))
+        work = ctx.enter_context(tc.tile_pool(name="work", bufs=4))
+        psum = ctx.enter_context(tc.psum_pool(name="psum", bufs=8))
+        ctx.enter_context(tc.manual_schedule())
+
+        ident = const.tile([P, P], F32, name="ident")
+        make_identity(nc, ident[:])
+
+        plane_k = const.tile([P, PASSES, 512], U8, name="plane_k", align_bytes=64)
+        plane_q = const.tile([P, PASSES, 2048], U8, name="plane_q", align_bytes=64)
+        plane_v = const.tile([P, PASSES, 512], U8, name="plane_v", align_bytes=64)
+        nc.vector.memset(plane_k[:].bitcast(I32), 0)
+
+        one = const.tile([P, 2], F32, name="one")
+        nc.vector.memset(one[:], 1.0)
+        warm = const.tile([P, 2], F32, name="warm")
+        nc.scalar.activation(out=warm[:], in_=one[:], func=ACT.Sin, scale=1.0)
+
+        pos_i = const.tile([P, TOKEN_TILES], I32, name="pos_i")
+        nc.gpsimd.iota(pos_i[:], pattern=[[P, TOKEN_TILES]], base=0, channel_multiplier=1)
+        phase = const.tile([P, PAIRS, 2], F32, name="phase")
+        nc.gpsimd.memset(phase[:], 0.0)
+        nc.gpsimd.memset(phase[:, :, 0:1], 0.25)
+        nc.gpsimd.memset(plane_q[:].bitcast(F32), 0.0)
+        nc.gpsimd.memset(plane_v[:].bitcast(F32), 0.0)
+
+        x_sb = [const.tile([P, 2048], BF16, name="x_sb%d" % t) for t in range(TOKEN_TILES)]
+        w_k = const.tile([P, PASSES, 1024], U8, name="w_k", align_bytes=64)
+        w_v = const.tile([P, PASSES, 1024], U8, name="w_v", align_bytes=64)
+        w_q = [const.tile([P, PASSES, 1024], U8, name="w_q%d" % n, align_bytes=64) for n in range(4)]
+
+        def load_x(t):
+            nc.sync.dma_start(out=x_sb[t][:], in_=x[P * t : P * (t + 1), :])
+
+        def load_scales(plane, scales):
+            for quad in range(4):
+                nc.sync.dma_start(
+                    out=plane[32 * quad : 32 * quad + 4, :, :].bitcast(I32),
+                    in_=scales[:, 4 * quad : 4 * quad + 4, :].rearrange("g r n -> r g n").bitcast(I32),
+                )
+
+        def load_words(tile, words):
+            nc.sync.dma_start(out=tile[:].bitcast(I32), in_=words.rearrange("g p c -> p g c").bitcast(I32))
+
+        load_x(0)
+        load_scales(plane_k, wk_scales)
+        load_x(1)
+        load_words(w_k, wk_words)
+        load_x(2)
+        load_x(3)
+        load_scales(plane_q, wq_scales)
+        for n in range(4):
+            load_words(w_q[n], wq_words[:, :, 1024 * n : 1024 * (n + 1)])
+        load_scales(plane_v, wv_scales)
+        load_words(w_v, wv_words)
+
+        freq = const.tile([P, PAIRS, 2], F32, name="freq")
+        freq_flat = freq[:].rearrange("p j e -> p (j e)")
+        nc.vector.tensor_scalar(
+            out=freq_flat[:, 0:2], in0=one[:], scalar1=1.0 / TWO_PI, scalar2=None, op0=ALU.mult
+        )
+        for i in range(6):
+            w = 2 << i
+            nc.vector.tensor_scalar(
+                out=freq_flat[:, w : 2 * w],
+                in0=freq_flat[:, 0:w],
+                scalar1=ROPE_THETA ** (-(1 << i) / 64.0),
+                scalar2=None,
+                op0=ALU.mult,
+            )
+        pos_f = const.tile([P, TOKEN_TILES], F32, name="pos_f")
+        nc.vector.tensor_copy(out=pos_f[:], in_=pos_i[:])
+        turns = const.tile([P, TOKEN_TILES, 2 * PAIRS], F32, name="turns")
+        for t in range(TOKEN_TILES):
+            nc.vector.scalar_tensor_tensor(
+                out=turns[:, t, :],
+                in0=freq_flat,
+                scalar=pos_f[:, t : t + 1],
+                in1=phase[:].rearrange("p j e -> p (j e)"),
+                op0=ALU.mult,
+                op1=ALU.add,
+            )
+        whole = const.tile([P, TOKEN_TILES, 2 * PAIRS], I32, name="whole")
+        nc.vector.tensor_copy(out=whole[:], in_=turns[:])
+        frac = const.tile([P, TOKEN_TILES, 2 * PAIRS], F32, name="frac")
+        nc.vector.tensor_tensor(out=frac[:], in0=turns[:], in1=whole[:], op=ALU.subtract)
+        tab_re = const.tile([P, TOKEN_TILES, PAIRS, 2], F32, name="tab_re")
+        tab_im = const.tile([P, TOKEN_TILES, PAIRS, 2], F32, name="tab_im")
+
+        def make_tables():
+            nc.scalar.activation(
+                out=tab_re[:].rearrange("p t j e -> p t (j e)"), in_=frac[:], func=ACT.Sin, scale=TWO_PI
+            )
+            nc.gpsimd.tensor_scalar(
+                out=tab_im[:, :, :, 0:1], in0=tab_re[:, :, :, 1:2], scalar1=-1.0, scalar2=0.0, op0=ALU.mult, op1=ALU.add
+            )
+            nc.gpsimd.tensor_scalar(
+                out=tab_im[:, :, :, 1:2], in0=tab_re[:, :, :, 0:1], scalar1=1.0, scalar2=0.0, op0=ALU.mult, op1=ALU.add
+            )
+
+        grouped = [const.tile([P, PASSES, P, 4], BF16, name="grouped%d" % t, align_bytes=64) for t in range(TOKEN_TILES)]
+        codes = [const.tile([P, PASSES, P], U32, name="codes%d" % t, align_bytes=64) for t in range(TOKEN_TILES)]
+        x_scales = [const.tile([P, PASSES, P], U8, name="x_scales%d" % t, align_bytes=64) for t in range(TOKEN_TILES)]
+
+        def transpose_tile(t):
+            words = x_sb[t][:].bitcast(F32)
+            for half in range(2):
+                xt = psum.tile([P, 2, 2, P], F32, name="xt", tag="bank")
+                for gg in range(2):
+                    g = 2 * half + gg
+                    for u in range(2):
+                        nc.tensor.transpose(xt[:, gg, u, :], words[:, 256 * g + u : 256 * (g + 1) : 2], ident[:])
+                nc.scalar.copy(
+                    out=grouped[t][:, 2 * half : 2 * half + 2, :, :].bitcast(F32),
+                    in_=xt[:].rearrange("p g u r -> p g r u"),
+                )
+
+        def quantise_tile(t):
+            for half in range(2):
+                gs = slice(2 * half, 2 * half + 2)
+                nc.vector.quantize_mx(
+                    out=codes[t][:, gs, :].rearrange("p g r -> p (g r)").bitcast(E5M2X4),
+                    scales=x_scales[t][:, gs, :].rearrange("p g r -> p (g r)"),
+                    in_=grouped[t][:, gs, :, :].rearrange("p g r j -> p (g r j)"),
+                )
+
+        blocks = [(w_k, plane_k, 0, k_out, 0, True)]
+        for n in range(4):
+            blocks.append((w_q[n], plane_q, N_TILE * n, q_out, N_TILE * n, True))
+        blocks.append((w_v, plane_v, 0, v_out, 0, False))
+
+        def multiply(b, t):
+            words, plane, plane_col = blocks[b][0], blocks[b][1], blocks[b][2]
+            acc = psum.tile([P, N_TILE], F32, name="acc", tag="bank")
+            for g in range(PASSES):
+                nc.tensor.matmul_mx(
+                    out=acc[:],
+                    lhsT=codes[t][:, g, :].bitcast(E5M2X4),
+                    lhsT_scale=x_scales[t][:, g, :],
+                    rhs=words[:, g, :].bitcast(E2M1X4),
+                    rhs_scale=plane[:, g, plane_col : plane_col + N_TILE],
+                    start=(g == 0),
+                    stop=(g == PASSES - 1),
+                )
+            return acc
+
+        def finish(b, t, acc):
+            dst, dst_col, rotate = blocks[b][3], blocks[b][4], blocks[b][5]
+            result = work.tile([P, N_TILE], F32, name="result", tag="result", bufs=6)
+            if rotate:
+                shape = [P, HEADS_PER_TILE, PAIRS, 2]
+                sums = acc[:].rearrange("p (h j e) -> p h j e", h=HEADS_PER_TILE, e=2)
+                from_re = work.tile([P, N_TILE], F32, name="from_re", tag="from_re")
+                from_im = work.tile([P, N_TILE], F32, name="from_im", tag="from_im")
+                nc.vector.tensor_tensor(
+                    out=from_re[:].rearrange("p (h j e) -> p h j e", h=HEADS_PER_TILE, e=2),
+                    in0=sums[:, :, :, 0:1].to_broadcast(shape),
+                    in1=tab_re[:, t, :, :].unsqueeze(1).to_broadcast(shape),
+                    op=ALU.mult,
+                )
+                nc.vector.tensor_tensor(
+                    out=from_im[:].rearrange("p (h j e) -> p h j e", h=HEADS_PER_TILE, e=2),
+                    in0=sums[:, :, :, 1:2].to_broadcast(shape),
+                    in1=tab_im[:, t, :, :].unsqueeze(1).to_broadcast(shape),
+                    op=ALU.mult,
+                )
+                nc.gpsimd.tensor_tensor(out=result[:], in0=from_re[:], in1=from_im[:], op=ALU.add)
+            else:
+                nc.scalar.copy(out=result[:], in_=acc[:])
+            nc.sync.dma_start(out=dst[P * t : P * (t + 1), dst_col : dst_col + N_TILE], in_=result[:])
+
+        transpose_tile(0)
+        transpose_tile(1)
+        quantise_tile(0)
+        acc0 = multiply(0, 0)
+        quantise_tile(1)
+        make_tables()
+        transpose_tile(2)
+        finish(0, 0, acc0)
+        acc1 = multiply(0, 1)
+        quantise_tile(2)
+        transpose_tile(3)
+        finish(0, 1, acc1)
+        acc2 = multiply(0, 2)
+        quantise_tile(3)
+        pending = (0, 2, acc2)
+        for b in range(len(blocks)):
+            for t in range(TOKEN_TILES):
+                if b == 0 and t < 3:
+                    continue
+                acc = multiply(b, t)
+                finish(pending[0], pending[1], pending[2])
+                pending = (b, t, acc)
+        finish(pending[0], pending[1], pending[2])

@@ -23,6 +23,9 @@ HEADS_PER_TILE = 4
 PAIRS = 64
 ROPE_THETA = 10000.0
 TWO_PI = 6.283185307179586
+WARM_UP = 4
+LAST_ROPE_BLOCK = 4
+PLANES = 3
 
 
 def tile_rptattention_pa_kernel(
@@ -41,33 +44,44 @@ def tile_rptattention_pa_kernel(
         ctx.enter_context(tc.manual_schedule())
 
         ident = const.tile([P, P], F32, name="ident")
-        make_identity(nc, ident[:])
-
-        plane_k = const.tile([P, PASSES, 512], U8, name="plane_k", align_bytes=64)
-        plane_q = const.tile([P, PASSES, 2048], U8, name="plane_q", align_bytes=64)
-        plane_v = const.tile([P, PASSES, 512], U8, name="plane_v", align_bytes=64)
-        nc.vector.memset(plane_k[:].bitcast(I32), 0)
-
+        idle_in = const.tile([P, N_TILE], BF16, name="idle_in")
+        planes = [const.tile([P, PASSES, N_TILE], U8, name="plane%d" % i, align_bytes=64) for i in range(PLANES)]
         one = const.tile([P, 2], F32, name="one")
-        nc.vector.memset(one[:], 1.0)
         warm = const.tile([P, 2], F32, name="warm")
-        nc.scalar.activation(out=warm[:], in_=one[:], func=ACT.Sin, scale=1.0)
-
         pos_i = const.tile([P, TOKEN_TILES], I32, name="pos_i")
-        nc.gpsimd.iota(pos_i[:], pattern=[[P, TOKEN_TILES]], base=0, channel_multiplier=1)
+        pos_f = const.tile([P, TOKEN_TILES], F32, name="pos_f")
         phase = const.tile([P, PAIRS, 2], F32, name="phase")
-        nc.gpsimd.memset(phase[:], 0.0)
-        nc.gpsimd.memset(phase[:, :, 0:1], 0.25)
-        nc.gpsimd.memset(plane_q[:].bitcast(F32), 0.0)
-        nc.gpsimd.memset(plane_v[:].bitcast(F32), 0.0)
-
-        x_sb = [const.tile([P, 2048], BF16, name="x_sb%d" % t) for t in range(TOKEN_TILES)]
+        freq = const.tile([P, 2 * PAIRS], F32, name="freq")
+        turns = const.tile([P, TOKEN_TILES, 2 * PAIRS], F32, name="turns")
+        whole = const.tile([P, TOKEN_TILES, 2 * PAIRS], I32, name="whole")
+        frac = const.tile([P, TOKEN_TILES, 2, PAIRS, 2], F32, name="frac")
+        table = const.tile([P, TOKEN_TILES, 2, PAIRS, 2], F32, name="table")
+        x_sb = [const.tile([P, 1024], BF16, name="x_sb%d" % i) for i in range(2 * TOKEN_TILES)]
         w_k = const.tile([P, PASSES, 1024], U8, name="w_k", align_bytes=64)
         w_v = const.tile([P, PASSES, 1024], U8, name="w_v", align_bytes=64)
         w_q = [const.tile([P, PASSES, 1024], U8, name="w_q%d" % n, align_bytes=64) for n in range(4)]
+        grouped = [const.tile([P, 2, P, 4], BF16, name="grouped%d" % i, align_bytes=64) for i in range(2 * TOKEN_TILES)]
+        codes = [const.tile([P, PASSES, P], U32, name="codes%d" % t, align_bytes=64) for t in range(TOKEN_TILES)]
+        x_scales = [const.tile([P, PASSES, P], U8, name="x_scales%d" % t, align_bytes=64) for t in range(TOKEN_TILES)]
 
-        def load_x(t):
-            nc.sync.dma_start(out=x_sb[t][:], in_=x[P * t : P * (t + 1), :])
+        nc.gpsimd.memset(idle_in[:], 0.0)
+        nc.vector.memset(planes[0][:].bitcast(I32), 0)
+        nc.vector.memset(one[:], 1.0)
+        nc.scalar.activation(out=warm[:], in_=one[:], func=ACT.Sin, scale=1.0)
+        make_identity(nc, ident[:])
+        nc.gpsimd.iota(pos_i[:], pattern=[[P, TOKEN_TILES]], base=0, channel_multiplier=1)
+
+        idle_out = psum.tile([P, N_TILE], F32, name="idle_out", tag="bank")
+
+        def idle_matmul():
+            nc.tensor.matmul(out=idle_out[:], lhsT=idle_in[:, 0:P], rhs=idle_in[:], start=True, stop=True)
+
+        for i in range(WARM_UP):
+            idle_matmul()
+
+        def load_x(i):
+            t, half = divmod(i, 2)
+            nc.sync.dma_start(out=x_sb[i][:], in_=x[P * t : P * (t + 1), 1024 * half : 1024 * (half + 1)])
 
         def load_scales(plane, scales):
             for quad in range(4):
@@ -76,98 +90,93 @@ def tile_rptattention_pa_kernel(
                     in_=scales[:, 4 * quad : 4 * quad + 4, :].rearrange("g r n -> r g n").bitcast(I32),
                 )
 
-        def load_words(tile, words):
-            nc.sync.dma_start(out=tile[:].bitcast(I32), in_=words.rearrange("g p c -> p g c").bitcast(I32))
+        def load_words(dst, words):
+            nc.sync.dma_start(out=dst[:].bitcast(I32), in_=words.rearrange("g p c -> p g c").bitcast(I32))
 
-        load_x(0)
-        load_scales(plane_k, wk_scales)
-        load_x(1)
+        for i in range(4):
+            load_x(i)
+        load_scales(planes[0], wk_scales)
         load_words(w_k, wk_words)
-        load_x(2)
-        load_x(3)
-        load_scales(plane_q, wq_scales)
-        for n in range(4):
-            load_words(w_q[n], wq_words[:, :, 1024 * n : 1024 * (n + 1)])
-        load_scales(plane_v, wv_scales)
-        load_words(w_v, wv_words)
+        for i in range(4, 8):
+            load_x(i)
 
-        freq = const.tile([P, PAIRS, 2], F32, name="freq")
-        freq_flat = freq[:].rearrange("p j e -> p (j e)")
-        nc.vector.tensor_scalar(
-            out=freq_flat[:, 0:2], in0=one[:], scalar1=1.0 / TWO_PI, scalar2=None, op0=ALU.mult
-        )
+        scale_rows = [wk_scales] + [wq_scales[:, :, N_TILE * n : N_TILE * (n + 1)] for n in range(4)] + [wv_scales]
+
+        nc.vector.tensor_scalar(out=freq[:, 0:2], in0=one[:], scalar1=1.0 / TWO_PI, scalar2=None, op0=ALU.mult)
         for i in range(6):
+            if i == 0 or i == 1:
+                nc.vector.memset(planes[i + 1][:].bitcast(I32), 0)
+            elif i == 2:
+                nc.vector.memset(phase[:], 0.0)
+            elif i == 3:
+                nc.vector.memset(phase[:, :, 0:1], 0.25)
             w = 2 << i
             nc.vector.tensor_scalar(
-                out=freq_flat[:, w : 2 * w],
-                in0=freq_flat[:, 0:w],
+                out=freq[:, w : 2 * w],
+                in0=freq[:, 0:w],
                 scalar1=ROPE_THETA ** (-(1 << i) / 64.0),
                 scalar2=None,
                 op0=ALU.mult,
             )
-        pos_f = const.tile([P, TOKEN_TILES], F32, name="pos_f")
+        load_scales(planes[1], scale_rows[1])
+        load_words(w_q[0], wq_words[:, :, 0:1024])
+        load_scales(planes[2], scale_rows[2])
+        load_words(w_q[1], wq_words[:, :, 1024:2048])
         nc.vector.tensor_copy(out=pos_f[:], in_=pos_i[:])
-        turns = const.tile([P, TOKEN_TILES, 2 * PAIRS], F32, name="turns")
         for t in range(TOKEN_TILES):
             nc.vector.scalar_tensor_tensor(
                 out=turns[:, t, :],
-                in0=freq_flat,
+                in0=freq[:],
                 scalar=pos_f[:, t : t + 1],
                 in1=phase[:].rearrange("p j e -> p (j e)"),
                 op0=ALU.mult,
                 op1=ALU.add,
             )
-        whole = const.tile([P, TOKEN_TILES, 2 * PAIRS], I32, name="whole")
         nc.vector.tensor_copy(out=whole[:], in_=turns[:])
-        frac = const.tile([P, TOKEN_TILES, 2 * PAIRS], F32, name="frac")
-        nc.vector.tensor_tensor(out=frac[:], in0=turns[:], in1=whole[:], op=ALU.subtract)
-        tab_re = const.tile([P, TOKEN_TILES, PAIRS, 2], F32, name="tab_re")
-        tab_im = const.tile([P, TOKEN_TILES, PAIRS, 2], F32, name="tab_im")
+
+        def fractions_for_re():
+            nc.vector.tensor_tensor(
+                out=frac[:, :, 0, :, :].rearrange("p t j e -> p t (j e)"), in0=turns[:], in1=whole[:], op=ALU.subtract
+            )
+
+        def fractions_for_im():
+            nc.vector.tensor_scalar(
+                out=frac[:, :, 1, :, 0:1], in0=frac[:, :, 0, :, 1:2], scalar1=-1.0, scalar2=None, op0=ALU.mult
+            )
+            nc.vector.tensor_copy(out=frac[:, :, 1, :, 1:2], in_=frac[:, :, 0, :, 0:1])
 
         def make_tables():
             nc.scalar.activation(
-                out=tab_re[:].rearrange("p t j e -> p t (j e)"), in_=frac[:], func=ACT.Sin, scale=TWO_PI
+                out=table[:].rearrange("p t a j e -> p (t a j e)"),
+                in_=frac[:].rearrange("p t a j e -> p (t a j e)"),
+                func=ACT.Sin,
+                scale=TWO_PI,
             )
-            nc.gpsimd.tensor_scalar(
-                out=tab_im[:, :, :, 0:1], in0=tab_re[:, :, :, 1:2], scalar1=-1.0, scalar2=0.0, op0=ALU.mult, op1=ALU.add
+        def transpose_half(i):
+            words = x_sb[i][:].bitcast(F32)
+            xt = psum.tile([P, 2, 2, P], F32, name="xt", tag="bank")
+            for gg in range(2):
+                for u in range(2):
+                    nc.tensor.transpose(xt[:, gg, u, :], words[:, 256 * gg + u : 256 * (gg + 1) : 2], ident[:])
+            nc.scalar.copy(out=grouped[i][:].bitcast(F32), in_=xt[:].rearrange("p g u r -> p g r u"))
+
+        def quantise_half(i):
+            t, half = divmod(i, 2)
+            gs = slice(2 * half, 2 * half + 2)
+            nc.vector.quantize_mx(
+                out=codes[t][:, gs, :].rearrange("p g r -> p (g r)").bitcast(E5M2X4),
+                scales=x_scales[t][:, gs, :].rearrange("p g r -> p (g r)"),
+                in_=grouped[i][:].rearrange("p g r j -> p (g r j)"),
             )
-            nc.gpsimd.tensor_scalar(
-                out=tab_im[:, :, :, 1:2], in0=tab_re[:, :, :, 0:1], scalar1=1.0, scalar2=0.0, op0=ALU.mult, op1=ALU.add
-            )
 
-        grouped = [const.tile([P, PASSES, P, 4], BF16, name="grouped%d" % t, align_bytes=64) for t in range(TOKEN_TILES)]
-        codes = [const.tile([P, PASSES, P], U32, name="codes%d" % t, align_bytes=64) for t in range(TOKEN_TILES)]
-        x_scales = [const.tile([P, PASSES, P], U8, name="x_scales%d" % t, align_bytes=64) for t in range(TOKEN_TILES)]
-
-        def transpose_tile(t):
-            words = x_sb[t][:].bitcast(F32)
-            for half in range(2):
-                xt = psum.tile([P, 2, 2, P], F32, name="xt", tag="bank")
-                for gg in range(2):
-                    g = 2 * half + gg
-                    for u in range(2):
-                        nc.tensor.transpose(xt[:, gg, u, :], words[:, 256 * g + u : 256 * (g + 1) : 2], ident[:])
-                nc.scalar.copy(
-                    out=grouped[t][:, 2 * half : 2 * half + 2, :, :].bitcast(F32),
-                    in_=xt[:].rearrange("p g u r -> p g r u"),
-                )
-
-        def quantise_tile(t):
-            for half in range(2):
-                gs = slice(2 * half, 2 * half + 2)
-                nc.vector.quantize_mx(
-                    out=codes[t][:, gs, :].rearrange("p g r -> p (g r)").bitcast(E5M2X4),
-                    scales=x_scales[t][:, gs, :].rearrange("p g r -> p (g r)"),
-                    in_=grouped[t][:, gs, :, :].rearrange("p g r j -> p (g r j)"),
-                )
-
-        blocks = [(w_k, plane_k, 0, k_out, 0, True)]
+        blocks = [(w_k, k_out, 0, True)]
         for n in range(4):
-            blocks.append((w_q[n], plane_q, N_TILE * n, q_out, N_TILE * n, True))
-        blocks.append((w_v, plane_v, 0, v_out, 0, False))
+            blocks.append((w_q[n], q_out, N_TILE * n, True))
+        blocks.append((w_v, v_out, 0, False))
 
         def multiply(b, t):
-            words, plane, plane_col = blocks[b][0], blocks[b][1], blocks[b][2]
+            words = blocks[b][0]
+            plane = planes[b % PLANES]
             acc = psum.tile([P, N_TILE], F32, name="acc", tag="bank")
             for g in range(PASSES):
                 nc.tensor.matmul_mx(
@@ -175,57 +184,83 @@ def tile_rptattention_pa_kernel(
                     lhsT=codes[t][:, g, :].bitcast(E5M2X4),
                     lhsT_scale=x_scales[t][:, g, :],
                     rhs=words[:, g, :].bitcast(E2M1X4),
-                    rhs_scale=plane[:, g, plane_col : plane_col + N_TILE],
+                    rhs_scale=plane[:, g, :],
                     start=(g == 0),
                     stop=(g == PASSES - 1),
                 )
             return acc
 
-        def finish(b, t, acc):
-            dst, dst_col, rotate = blocks[b][3], blocks[b][4], blocks[b][5]
-            result = work.tile([P, N_TILE], F32, name="result", tag="result", bufs=6)
-            if rotate:
-                shape = [P, HEADS_PER_TILE, PAIRS, 2]
-                sums = acc[:].rearrange("p (h j e) -> p h j e", h=HEADS_PER_TILE, e=2)
-                from_re = work.tile([P, N_TILE], F32, name="from_re", tag="from_re")
-                from_im = work.tile([P, N_TILE], F32, name="from_im", tag="from_im")
-                nc.vector.tensor_tensor(
-                    out=from_re[:].rearrange("p (h j e) -> p h j e", h=HEADS_PER_TILE, e=2),
-                    in0=sums[:, :, :, 0:1].to_broadcast(shape),
-                    in1=tab_re[:, t, :, :].unsqueeze(1).to_broadcast(shape),
-                    op=ALU.mult,
-                )
-                nc.vector.tensor_tensor(
-                    out=from_im[:].rearrange("p (h j e) -> p h j e", h=HEADS_PER_TILE, e=2),
-                    in0=sums[:, :, :, 1:2].to_broadcast(shape),
-                    in1=tab_im[:, t, :, :].unsqueeze(1).to_broadcast(shape),
-                    op=ALU.mult,
-                )
-                nc.gpsimd.tensor_tensor(out=result[:], in0=from_re[:], in1=from_im[:], op=ALU.add)
-            else:
-                nc.scalar.copy(out=result[:], in_=acc[:])
-            nc.sync.dma_start(out=dst[P * t : P * (t + 1), dst_col : dst_col + N_TILE], in_=result[:])
+        def new_pair():
+            from_re = work.tile([P, 2, N_TILE], F32, name="from_re", tag="from_re")
+            from_im = work.tile([P, 2, N_TILE], F32, name="from_im", tag="from_im")
+            return (from_re, from_im)
 
-        transpose_tile(0)
-        transpose_tile(1)
-        quantise_tile(0)
-        acc0 = multiply(0, 0)
-        quantise_tile(1)
+        def finish(b, t, acc, pair):
+            dst, dst_col, rotate = blocks[b][1], blocks[b][2], blocks[b][3]
+            if not rotate:
+                v_result = work.tile([P, N_TILE], F32, name="v_result", tag="v_result")
+                nc.scalar.copy(out=v_result[:], in_=acc[:])
+                nc.scalar.dma_start(out=dst[P * t : P * (t + 1), dst_col : dst_col + N_TILE], in_=v_result[:])
+                return
+            s = t % 2
+            shape = [P, HEADS_PER_TILE, PAIRS, 2]
+            sums = acc[:].rearrange("p (h j e) -> p h j e", h=HEADS_PER_TILE, e=2)
+            for part in range(2):
+                nc.vector.tensor_tensor(
+                    out=pair[part][:, s, :].rearrange("p (h j e) -> p h j e", h=HEADS_PER_TILE, e=2),
+                    in0=sums[:, :, :, part : part + 1].to_broadcast(shape),
+                    in1=table[:, t, part, :, :].unsqueeze(1).to_broadcast(shape),
+                    op=ALU.mult,
+                )
+            if s == 1:
+                result = work.tile([P, 2, N_TILE], F32, name="result", tag="result")
+                adder = nc.vector if (b == LAST_ROPE_BLOCK and t == TOKEN_TILES - 1) else nc.gpsimd
+                adder.tensor_tensor(out=result[:], in0=pair[0][:], in1=pair[1][:], op=ALU.add)
+                nc.sync.dma_start(
+                    out=dst[P * (t - 1) : P * (t + 1), dst_col : dst_col + N_TILE].rearrange("(s p) c -> p s c", p=P),
+                    in_=result[:],
+                )
+
+        transpose_half(0)
+        idle_matmul()
+        transpose_half(1)
+        idle_matmul()
+        transpose_half(2)
+        idle_matmul()
+        transpose_half(3)
+        idle_matmul()
+        quantise_half(0)
+        fractions_for_re()
+        quantise_half(1)
+        fractions_for_im()
         make_tables()
-        transpose_tile(2)
-        finish(0, 0, acc0)
+        quantise_half(2)
+        quantise_half(3)
+        acc0 = multiply(0, 0)
+        for i in range(4, 8):
+            transpose_half(i)
+        pair = new_pair()
+        finish(0, 0, acc0, pair)
+        for i in range(4, 8):
+            quantise_half(i)
         acc1 = multiply(0, 1)
-        quantise_tile(2)
-        transpose_tile(3)
-        finish(0, 1, acc1)
         acc2 = multiply(0, 2)
-        quantise_tile(3)
+        finish(0, 1, acc1, pair)
+        load_words(w_q[2], wq_words[:, :, 2048:3072])
         pending = (0, 2, acc2)
         for b in range(len(blocks)):
             for t in range(TOKEN_TILES):
                 if b == 0 and t < 3:
                     continue
                 acc = multiply(b, t)
-                finish(pending[0], pending[1], pending[2])
+                if pending[1] % 2 == 0 and blocks[pending[0]][3]:
+                    pair = new_pair()
+                finish(pending[0], pending[1], pending[2], pair)
+                if pending[1] == TOKEN_TILES - 1 and pending[0] + PLANES < len(blocks):
+                    load_scales(planes[pending[0] % PLANES], scale_rows[pending[0] + PLANES])
+                    if pending[0] == 0:
+                        load_words(w_q[3], wq_words[:, :, 3072:4096])
+                    if pending[0] == 1:
+                        load_words(w_v, wv_words)
                 pending = (b, t, acc)
-        finish(pending[0], pending[1], pending[2])
+        finish(pending[0], pending[1], pending[2], pair)

@@ -191,31 +191,35 @@ def tile_rptattention_pa_kernel(
             return acc
 
         def new_pair():
-            from_re = work.tile([P, 2, N_TILE], F32, name="from_re", tag="from_re")
-            from_im = work.tile([P, 2, N_TILE], F32, name="from_im", tag="from_im")
-            return (from_re, from_im)
+            products = work.tile([P, 2, 2, N_TILE], F32, name="products", tag="products")
+            return products
 
         def finish(b, t, acc, pair):
             dst, dst_col, rotate = blocks[b][1], blocks[b][2], blocks[b][3]
             if not rotate:
-                v_result = work.tile([P, N_TILE], F32, name="v_result", tag="v_result")
-                nc.scalar.copy(out=v_result[:], in_=acc[:])
-                nc.scalar.dma_start(out=dst[P * t : P * (t + 1), dst_col : dst_col + N_TILE], in_=v_result[:])
+                pieces = 2 if t == TOKEN_TILES - 1 else 1
+                width = N_TILE // pieces
+                for piece in range(pieces):
+                    v_result = work.tile([P, width], F32, name="v_result", tag="v_result", bufs=5)
+                    nc.scalar.copy(out=v_result[:], in_=acc[:, width * piece : width * (piece + 1)])
+                    queue = nc.sync if pieces - piece == 2 else nc.scalar
+                    queue.dma_start(
+                        out=dst[P * t : P * (t + 1), dst_col + width * piece : dst_col + width * (piece + 1)],
+                        in_=v_result[:],
+                    )
                 return
             s = t % 2
-            shape = [P, HEADS_PER_TILE, PAIRS, 2]
-            sums = acc[:].rearrange("p (h j e) -> p h j e", h=HEADS_PER_TILE, e=2)
-            for part in range(2):
-                nc.vector.tensor_tensor(
-                    out=pair[part][:, s, :].rearrange("p (h j e) -> p h j e", h=HEADS_PER_TILE, e=2),
-                    in0=sums[:, :, :, part : part + 1].to_broadcast(shape),
-                    in1=table[:, t, part, :, :].unsqueeze(1).to_broadcast(shape),
-                    op=ALU.mult,
-                )
+            shape = [P, 2, HEADS_PER_TILE, PAIRS, 2]
+            nc.vector.tensor_tensor(
+                out=pair[:, :, s, :].rearrange("p a (h j e) -> p a h j e", h=HEADS_PER_TILE, e=2),
+                in0=acc[:].rearrange("p (h j a) -> p a h j", h=HEADS_PER_TILE, a=2).unsqueeze(4).to_broadcast(shape),
+                in1=table[:, t, :, :, :].unsqueeze(2).to_broadcast(shape),
+                op=ALU.mult,
+            )
             if s == 1:
                 result = work.tile([P, 2, N_TILE], F32, name="result", tag="result")
                 adder = nc.vector if (b == LAST_ROPE_BLOCK and t == TOKEN_TILES - 1) else nc.gpsimd
-                adder.tensor_tensor(out=result[:], in0=pair[0][:], in1=pair[1][:], op=ALU.add)
+                adder.tensor_tensor(out=result[:], in0=pair[:, 0, :, :], in1=pair[:, 1, :, :], op=ALU.add)
                 nc.sync.dma_start(
                     out=dst[P * (t - 1) : P * (t + 1), dst_col : dst_col + N_TILE].rearrange("(s p) c -> p s c", p=P),
                     in_=result[:],

@@ -45,7 +45,7 @@ def tile_rptattention_pa_kernel(
 
         ident = const.tile([P, P], F32, name="ident")
         idle_in = const.tile([P, N_TILE], BF16, name="idle_in")
-        planes = [const.tile([P, PASSES, N_TILE], U8, name="plane%d" % i, align_bytes=64) for i in range(PLANES)]
+        planes = [const.tile([P, PASSES, N_TILE], U8, name="plane%d" % i, align_bytes=256) for i in range(PLANES)]
         one = const.tile([P, 2], F32, name="one")
         warm = const.tile([P, 2], F32, name="warm")
         pos_i = const.tile([P, TOKEN_TILES], I32, name="pos_i")
@@ -57,12 +57,12 @@ def tile_rptattention_pa_kernel(
         frac = const.tile([P, TOKEN_TILES, 2, PAIRS, 2], F32, name="frac")
         table = const.tile([P, TOKEN_TILES, 2, PAIRS, 2], F32, name="table")
         x_sb = [const.tile([P, 1024], BF16, name="x_sb%d" % i) for i in range(2 * TOKEN_TILES)]
-        w_k = const.tile([P, PASSES, 1024], U8, name="w_k", align_bytes=64)
-        w_v = const.tile([P, PASSES, 1024], U8, name="w_v", align_bytes=64)
-        w_q = [const.tile([P, PASSES, 1024], U8, name="w_q%d" % n, align_bytes=64) for n in range(4)]
-        grouped = [const.tile([P, 2, P, 4], BF16, name="grouped%d" % i, align_bytes=64) for i in range(2 * TOKEN_TILES)]
-        codes = [const.tile([P, PASSES, P], U32, name="codes%d" % t, align_bytes=64) for t in range(TOKEN_TILES)]
-        x_scales = [const.tile([P, PASSES, P], U8, name="x_scales%d" % t, align_bytes=64) for t in range(TOKEN_TILES)]
+        w_k = const.tile([P, PASSES, 1024], U8, name="w_k", align_bytes=256)
+        w_v = const.tile([P, PASSES, 1024], U8, name="w_v", align_bytes=256)
+        w_q = [const.tile([P, PASSES, 1024], U8, name="w_q%d" % n, align_bytes=256) for n in range(4)]
+        grouped = [const.tile([P, 2, P, 4], BF16, name="grouped%d" % i, align_bytes=256) for i in range(2 * TOKEN_TILES)]
+        codes = [const.tile([P, PASSES, P], U32, name="codes%d" % t, align_bytes=256) for t in range(TOKEN_TILES)]
+        x_scales = [const.tile([P, PASSES, P], U8, name="x_scales%d" % t, align_bytes=256) for t in range(TOKEN_TILES)]
 
         nc.gpsimd.memset(idle_in[:], 0.0)
         nc.vector.memset(planes[0][:].bitcast(I32), 0)

@@ -194,6 +194,17 @@ def tile_rptattention_pa_kernel(
             products = work.tile([P, 2, 2, N_TILE], F32, name="products", tag="products")
             return products
 
+        def combine(adder, b, t, pair):
+            dst, dst_col = blocks[b][1], blocks[b][2]
+            result = work.tile([P, 2, N_TILE], F32, name="result", tag="result")
+            adder.tensor_tensor(out=result[:], in0=pair[:, 0, :, :], in1=pair[:, 1, :, :], op=ALU.add)
+            nc.sync.dma_start(
+                out=dst[P * (t - 1) : P * (t + 1), dst_col : dst_col + N_TILE].rearrange("(s p) c -> p s c", p=P),
+                in_=result[:],
+            )
+
+        held = []
+
         def finish(b, t, acc, pair):
             dst, dst_col, rotate = blocks[b][1], blocks[b][2], blocks[b][3]
             if not rotate:
@@ -216,14 +227,13 @@ def tile_rptattention_pa_kernel(
                 in1=table[:, t, :, :, :].unsqueeze(2).to_broadcast(shape),
                 op=ALU.mult,
             )
-            if s == 1:
-                result = work.tile([P, 2, N_TILE], F32, name="result", tag="result")
-                adder = nc.vector if (b == LAST_ROPE_BLOCK and t == TOKEN_TILES - 1) else nc.gpsimd
-                adder.tensor_tensor(out=result[:], in0=pair[:, 0, :, :], in1=pair[:, 1, :, :], op=ALU.add)
-                nc.sync.dma_start(
-                    out=dst[P * (t - 1) : P * (t + 1), dst_col : dst_col + N_TILE].rearrange("(s p) c -> p s c", p=P),
-                    in_=result[:],
-                )
+            if s == 1 and b < LAST_ROPE_BLOCK:
+                combine(nc.gpsimd, b, t, pair)
+            elif s == 1:
+                held.append(pair)
+                if t == TOKEN_TILES - 1:
+                    combine(nc.vector, b, 1, held[0])
+                    combine(nc.vector, b, 3, held[1])
 
         transpose_half(0)
         idle_matmul()
@@ -257,14 +267,14 @@ def tile_rptattention_pa_kernel(
                 if b == 0 and t < 3:
                     continue
                 acc = multiply(b, t)
+                if t == TOKEN_TILES - 1 and b + PLANES < len(blocks):
+                    load_scales(planes[b % PLANES], scale_rows[b + PLANES])
+                    if b == 0:
+                        load_words(w_q[3], wq_words[:, :, 3072:4096])
+                    if b == 1:
+                        load_words(w_v, wv_words)
                 if pending[1] % 2 == 0 and blocks[pending[0]][3]:
                     pair = new_pair()
                 finish(pending[0], pending[1], pending[2], pair)
-                if pending[1] == TOKEN_TILES - 1 and pending[0] + PLANES < len(blocks):
-                    load_scales(planes[pending[0] % PLANES], scale_rows[pending[0] + PLANES])
-                    if pending[0] == 0:
-                        load_words(w_q[3], wq_words[:, :, 3072:4096])
-                    if pending[0] == 1:
-                        load_words(w_v, wv_words)
                 pending = (b, t, acc)
         finish(pending[0], pending[1], pending[2], pair)

@@ -96,7 +96,11 @@ def tile_rptattention_pa_kernel(
         for i in range(4):
             load_x(i)
         load_scales(planes[0], wk_scales)
-        load_words(w_k, wk_words)
+        for first in (0, 2):
+            nc.sync.dma_start(
+                out=w_k[:, first : first + 2, :].bitcast(I32),
+                in_=wk_words[first : first + 2].rearrange("g p c -> p g c").bitcast(I32),
+            )
         for i in range(4, 8):
             load_x(i)
 
@@ -233,16 +237,19 @@ def tile_rptattention_pa_kernel(
                 held.append(pair)
                 if t == TOKEN_TILES - 1:
                     combine(nc.vector, b, 1, held[0])
-                    combine(nc.vector, b, 3, held[1])
+                    for half in range(2):
+                        last = work.tile([P, N_TILE], F32, name="last", tag="last", bufs=2)
+                        nc.vector.tensor_tensor(out=last[:], in0=held[1][:, 0, half, :], in1=held[1][:, 1, half, :], op=ALU.add)
+                        nc.sync.dma_start(
+                            out=dst[P * (2 + half) : P * (3 + half), dst_col : dst_col + N_TILE], in_=last[:]
+                        )
 
         transpose_half(0)
         idle_matmul()
         transpose_half(1)
         idle_matmul()
         transpose_half(2)
-        idle_matmul()
         transpose_half(3)
-        idle_matmul()
         quantise_half(0)
         fractions_for_re()
         quantise_half(1)

@@ -149,10 +149,10 @@ def tile_rptattention_pa_kernel(
             )
             nc.vector.tensor_copy(out=frac[:, :, 1, :, 1:2], in_=frac[:, :, 0, :, 0:1])
 
-        def make_tables():
+        def make_tables(first, last):
             nc.scalar.activation(
-                out=table[:].rearrange("p t a j e -> p (t a j e)"),
-                in_=frac[:].rearrange("p t a j e -> p (t a j e)"),
+                out=table[:, first:last].rearrange("p t a j e -> p (t a j e)"),
+                in_=frac[:, first:last].rearrange("p t a j e -> p (t a j e)"),
                 func=ACT.Sin,
                 scale=TWO_PI,
             )
@@ -202,12 +202,11 @@ def tile_rptattention_pa_kernel(
             dst, dst_col = blocks[b][1], blocks[b][2]
             result = work.tile([P, 2, N_TILE], F32, name="result", tag="result")
             adder.tensor_tensor(out=result[:], in0=pair[:, 0, :, :], in1=pair[:, 1, :, :], op=ALU.add)
-            nc.sync.dma_start(
+            queue = nc.scalar if b < PLANES else nc.sync
+            queue.dma_start(
                 out=dst[P * (t - 1) : P * (t + 1), dst_col : dst_col + N_TILE].rearrange("(s p) c -> p s c", p=P),
                 in_=result[:],
             )
-
-        held = []
 
         def finish(b, t, acc, pair):
             dst, dst_col, rotate = blocks[b][1], blocks[b][2], blocks[b][3]
@@ -233,16 +232,13 @@ def tile_rptattention_pa_kernel(
             )
             if s == 1 and b < LAST_ROPE_BLOCK:
                 combine(nc.gpsimd, b, t, pair)
+            elif s == 1 and t == 1:
+                combine(nc.vector, b, t, pair)
             elif s == 1:
-                held.append(pair)
-                if t == TOKEN_TILES - 1:
-                    combine(nc.vector, b, 1, held[0])
-                    for half in range(2):
-                        last = work.tile([P, N_TILE], F32, name="last", tag="last", bufs=2)
-                        nc.vector.tensor_tensor(out=last[:], in0=held[1][:, 0, half, :], in1=held[1][:, 1, half, :], op=ALU.add)
-                        nc.sync.dma_start(
-                            out=dst[P * (2 + half) : P * (3 + half), dst_col : dst_col + N_TILE], in_=last[:]
-                        )
+                for half in range(2):
+                    last = work.tile([P, N_TILE], F32, name="last", tag="last", bufs=2)
+                    nc.vector.tensor_tensor(out=last[:], in0=pair[:, 0, half, :], in1=pair[:, 1, half, :], op=ALU.add)
+                    nc.sync.dma_start(out=dst[P * (2 + half) : P * (3 + half), dst_col : dst_col + N_TILE], in_=last[:])
 
         transpose_half(0)
         idle_matmul()
@@ -254,7 +250,8 @@ def tile_rptattention_pa_kernel(
         fractions_for_re()
         quantise_half(1)
         fractions_for_im()
-        make_tables()
+        make_tables(0, 1)
+        make_tables(1, TOKEN_TILES)
         quantise_half(2)
         quantise_half(3)
         acc0 = multiply(0, 0)
@@ -269,19 +266,18 @@ def tile_rptattention_pa_kernel(
         finish(0, 1, acc1, pair)
         load_words(w_q[2], wq_words[:, :, 2048:3072])
         pending = (0, 2, acc2)
-        for b in range(len(blocks)):
-            for t in range(TOKEN_TILES):
-                if b == 0 and t < 3:
-                    continue
-                acc = multiply(b, t)
-                if t == TOKEN_TILES - 1 and b + PLANES < len(blocks):
-                    load_scales(planes[b % PLANES], scale_rows[b + PLANES])
-                    if b == 0:
-                        load_words(w_q[3], wq_words[:, :, 3072:4096])
-                    if b == 1:
-                        load_words(w_v, wv_words)
-                if pending[1] % 2 == 0 and blocks[pending[0]][3]:
-                    pair = new_pair()
-                finish(pending[0], pending[1], pending[2], pair)
-                pending = (b, t, acc)
+        order = [(0, 3)] + [(b, t) for b in range(1, LAST_ROPE_BLOCK) for t in range(TOKEN_TILES)]
+        order.extend([(4, 0), (4, 1), (5, 0), (4, 2), (4, 3), (5, 1), (5, 2), (5, 3)])
+        for b, t in order:
+            acc = multiply(b, t)
+            if t == TOKEN_TILES - 1 and b + PLANES < len(blocks):
+                load_scales(planes[b % PLANES], scale_rows[b + PLANES])
+                if b == 0:
+                    load_words(w_q[3], wq_words[:, :, 3072:4096])
+                if b == 1:
+                    load_words(w_v, wv_words)
+            if pending[1] % 2 == 0 and blocks[pending[0]][3]:
+                pair = new_pair()
+            finish(pending[0], pending[1], pending[2], pair)
+            pending = (b, t, acc)
         finish(pending[0], pending[1], pending[2], pair)

@@ -245,7 +245,9 @@ def tile_rptattention_pa_kernel(
         transpose_half(1)
         idle_matmul()
         transpose_half(2)
+        idle_matmul()
         transpose_half(3)
+        idle_matmul()
         quantise_half(0)
         fractions_for_re()
         quantise_half(1)

from contextlib import ExitStack

import concourse.mybir as mybir
from concourse.masks import make_identity

FLOPS = 2 * 512 * 2048 * 3072

F32 = mybir.dt.float32
BF16 = mybir.dt.bfloat16
I32 = mybir.dt.int32
U32 = mybir.dt.uint32
U8 = mybir.dt.uint8
E5M2X4 = mybir.dt.float8_e5m2_x4
E2M1X4 = mybir.dt.float4_e2m1fn_x4
ALU = mybir.AluOpType
ACT = mybir.ActivationFunctionType

P = 128
TOKEN_TILES = 4
PASSES = 4
N_TILE = 512
HEADS_PER_TILE = 4
PAIRS = 64
ROPE_THETA = 10000.0
TWO_PI = 6.283185307179586
WARM_UP = 4
LAST_ROPE_BLOCK = 4
PLANES = 3


def tile_rptattention_pa_kernel(
    tc, hidden_states, wq_words, wq_scales, wk_words, wk_scales, wv_words, wv_scales, out_0, out_1, out_2
):
    nc = tc.nc
    x = hidden_states.flatten_outer_dims()
    q_out = out_0.rearrange("b s h d -> (b s) (h d)")
    k_out = out_1.rearrange("b s h d -> (b s) (h d)")
    v_out = out_2.rearrange("b s h d -> (b s) (h d)")

    with ExitStack() as ctx:
        const = ctx.enter_context(tc.tile_pool(name="const", bufs=1))
        work = ctx.enter_context(tc.tile_pool(name="work", bufs=4))
        psum = ctx.enter_context(tc.psum_pool(name="psum", bufs=8))
        ctx.enter_context(tc.manual_schedule())

        ident = const.tile([P, P], F32, name="ident")
        idle_in = const.tile([P, N_TILE], BF16, name="idle_in")
        planes = [const.tile([P, PASSES, N_TILE], U8, name="plane%d" % i, align_bytes=256) for i in range(PLANES)]
        one = const.tile([P, 2], F32, name="one")
        warm = const.tile([P, 2], F32, name="warm")
        pos_i = const.tile([P, TOKEN_TILES], I32, name="pos_i")
        pos_f = const.tile([P, TOKEN_TILES], F32, name="pos_f")
        phase = const.tile([P, PAIRS, 2], F32, name="phase")
        freq = const.tile([P, 2 * PAIRS], F32, name="freq")
        turns = const.tile([P, TOKEN_TILES, 2 * PAIRS], F32, name="turns")
        whole = const.tile([P, TOKEN_TILES, 2 * PAIRS], I32, name="whole")
        frac = const.tile([P, TOKEN_TILES, 2, PAIRS, 2], F32, name="frac")
        table = const.tile([P, TOKEN_TILES, 2, PAIRS, 2], F32, name="table")
        x_sb = [const.tile([P, 1024], BF16, name="x_sb%d" % i) for i in range(2 * TOKEN_TILES)]
        w_k = const.tile([P, PASSES, 1024], U8, name="w_k", align_bytes=256)
        w_v = const.tile([P, PASSES, 1024], U8, name="w_v", align_bytes=256)
        w_q = [const.tile([P, PASSES, 1024], U8, name="w_q%d" % n, align_bytes=256) for n in range(4)]
        grouped = [const.tile([P, 2, P, 4], BF16, name="grouped%d" % i, align_bytes=256) for i in range(2 * TOKEN_TILES)]
        codes = [const.tile([P, PASSES, P], U32, name="codes%d" % t, align_bytes=256) for t in range(TOKEN_TILES)]
        x_scales = [const.tile([P, PASSES, P], U8, name="x_scales%d" % t, align_bytes=256) for t in range(TOKEN_TILES)]

        nc.gpsimd.memset(idle_in[:], 0.0)
        nc.vector.memset(planes[0][:].bitcast(I32), 0)
        nc.vector.memset(one[:], 1.0)
        nc.scalar.activation(out=warm[:], in_=one[:], func=ACT.Sin, scale=1.0)
        make_identity(nc, ident[:])
        nc.gpsimd.iota(pos_i[:], pattern=[[P, TOKEN_TILES]], base=0, channel_multiplier=1)

        idle_out = psum.tile([P, N_TILE], F32, name="idle_out", tag="bank")

        def idle_matmul():
            nc.tensor.matmul(out=idle_out[:], lhsT=idle_in[:, 0:P], rhs=idle_in[:], start=True, stop=True)

        for i in range(WARM_UP):
            idle_matmul()

        def load_x(i):
            t, half = divmod(i, 2)
            nc.sync.dma_start(out=x_sb[i][:], in_=x[P * t : P * (t + 1), 1024 * half : 1024 * (half + 1)])

        def load_scales(plane, scales):
            for quad in range(4):
                nc.sync.dma_start(
                    out=plane[32 * quad : 32 * quad + 4, :, :].bitcast(I32),
                    in_=scales[:, 4 * quad : 4 * quad + 4, :].rearrange("g r n -> r g n").bitcast(I32),
                )

        def load_words(dst, words):
            nc.sync.dma_start(out=dst[:].bitcast(I32), in_=words.rearrange("g p c -> p g c").bitcast(I32))

        for i in range(4):
            load_x(i)
        load_scales(planes[0], wk_scales)
        for first in (0, 2):
            nc.sync.dma_start(
                out=w_k[:, first : first + 2, :].bitcast(I32),
                in_=wk_words[first : first + 2].rearrange("g p c -> p g c").bitcast(I32),
            )
        for i in range(4, 8):
            load_x(i)

        scale_rows = [wk_scales] + [wq_scales[:, :, N_TILE * n : N_TILE * (n + 1)] for n in range(4)] + [wv_scales]

        nc.vector.tensor_scalar(out=freq[:, 0:2], in0=one[:], scalar1=1.0 / TWO_PI, scalar2=None, op0=ALU.mult)
        for i in range(6):
            if i == 0 or i == 1:
                nc.vector.memset(planes[i + 1][:].bitcast(I32), 0)
            elif i == 2:
                nc.vector.memset(phase[:], 0.0)
            elif i == 3:
                nc.vector.memset(phase[:, :, 0:1], 0.25)
            w = 2 << i
            nc.vector.tensor_scalar(
                out=freq[:, w : 2 * w],
                in0=freq[:, 0:w],
                scalar1=ROPE_THETA ** (-(1 << i) / 64.0),
                scalar2=None,
                op0=ALU.mult,
            )
        load_scales(planes[1], scale_rows[1])
        load_words(w_q[0], wq_words[:, :, 0:1024])
        load_scales(planes[2], scale_rows[2])
        load_words(w_q[1], wq_words[:, :, 1024:2048])
        nc.vector.tensor_copy(out=pos_f[:], in_=pos_i[:])
        for t in range(TOKEN_TILES):
            nc.vector.scalar_tensor_tensor(
                out=turns[:, t, :],
                in0=freq[:],
                scalar=pos_f[:, t : t + 1],
                in1=phase[:].rearrange("p j e -> p (j e)"),
                op0=ALU.mult,
                op1=ALU.add,
            )
        nc.vector.tensor_copy(out=whole[:], in_=turns[:])

        def fractions_for_re():
            nc.vector.tensor_tensor(
                out=frac[:, :, 0, :, :].rearrange("p t j e -> p t (j e)"), in0=turns[:], in1=whole[:], op=ALU.subtract
            )

        def fractions_for_im():
            nc.vector.tensor_scalar(
                out=frac[:, :, 1, :, 0:1], in0=frac[:, :, 0, :, 1:2], scalar1=-1.0, scalar2=None, op0=ALU.mult
            )
            nc.vector.tensor_copy(out=frac[:, :, 1, :, 1:2], in_=frac[:, :, 0, :, 0:1])

        def make_tables(first, last):
            nc.scalar.activation(
                out=table[:, first:last].rearrange("p t a j e -> p (t a j e)"),
                in_=frac[:, first:last].rearrange("p t a j e -> p (t a j e)"),
                func=ACT.Sin,
                scale=TWO_PI,
            )
        def transpose_half(i):
            words = x_sb[i][:].bitcast(F32)
            xt = psum.tile([P, 2, 2, P], F32, name="xt", tag="bank")
            for gg in range(2):
                for u in range(2):
                    nc.tensor.transpose(xt[:, gg, u, :], words[:, 256 * gg + u : 256 * (gg + 1) : 2], ident[:])
            nc.scalar.copy(out=grouped[i][:].bitcast(F32), in_=xt[:].rearrange("p g u r -> p g r u"))

        def quantise_half(i):
            t, half = divmod(i, 2)
            gs = slice(2 * half, 2 * half + 2)
            nc.vector.quantize_mx(
                out=codes[t][:, gs, :].rearrange("p g r -> p (g r)").bitcast(E5M2X4),
                scales=x_scales[t][:, gs, :].rearrange("p g r -> p (g r)"),
                in_=grouped[i][:].rearrange("p g r j -> p (g r j)"),
            )

        blocks = [(w_k, k_out, 0, True)]
        for n in range(4):
            blocks.append((w_q[n], q_out, N_TILE * n, True))
        blocks.append((w_v, v_out, 0, False))

        def multiply(b, t):
            words = blocks[b][0]
            plane = planes[b % PLANES]
            acc = psum.tile([P, N_TILE], F32, name="acc", tag="bank")
            for g in range(PASSES):
                nc.tensor.matmul_mx(
                    out=acc[:],
                    lhsT=codes[t][:, g, :].bitcast(E5M2X4),
                    lhsT_scale=x_scales[t][:, g, :],
                    rhs=words[:, g, :].bitcast(E2M1X4),
                    rhs_scale=plane[:, g, :],
                    start=(g == 0),
                    stop=(g == PASSES - 1),
                )
            return acc

        def new_pair():
            products = work.tile([P, 2, 2, N_TILE], F32, name="products", tag="products")
            return products

        def combine(adder, b, t, pair):
            dst, dst_col = blocks[b][1], blocks[b][2]
            result = work.tile([P, 2, N_TILE], F32, name="result", tag="result")
            adder.tensor_tensor(out=result[:], in0=pair[:, 0, :, :], in1=pair[:, 1, :, :], op=ALU.add)
            queue = nc.scalar if b < PLANES else nc.sync
            queue.dma_start(
                out=dst[P * (t - 1) : P * (t + 1), dst_col : dst_col + N_TILE].rearrange("(s p) c -> p s c", p=P),
                in_=result[:],
            )

        def finish(b, t, acc, pair):
            dst, dst_col, rotate = blocks[b][1], blocks[b][2], blocks[b][3]
            if not rotate:
                pieces = 2 if t == TOKEN_TILES - 1 else 1
                width = N_TILE // pieces
                for piece in range(pieces):
                    v_result = work.tile([P, width], F32, name="v_result", tag="v_result", bufs=5)
                    nc.scalar.copy(out=v_result[:], in_=acc[:, width * piece : width * (piece + 1)])
                    queue = nc.sync if pieces - piece == 2 else nc.scalar
                    queue.dma_start(
                        out=dst[P * t : P * (t + 1), dst_col + width * piece : dst_col + width * (piece + 1)],
                        in_=v_result[:],
                    )
                return
            s = t % 2
            shape = [P, 2, HEADS_PER_TILE, PAIRS, 2]
            nc.vector.tensor_tensor(
                out=pair[:, :, s, :].rearrange("p a (h j e) -> p a h j e", h=HEADS_PER_TILE, e=2),
                in0=acc[:].rearrange("p (h j a) -> p a h j", h=HEADS_PER_TILE, a=2).unsqueeze(4).to_broadcast(shape),
                in1=table[:, t, :, :, :].unsqueeze(2).to_broadcast(shape),
                op=ALU.mult,
            )
            if s == 1 and b < LAST_ROPE_BLOCK:
                combine(nc.gpsimd, b, t, pair)
            elif s == 1 and t == 1:
                combine(nc.vector, b, t, pair)
            elif s == 1:
                for half in range(2):
                    last = work.tile([P, N_TILE], F32, name="last", tag="last", bufs=2)
                    nc.vector.tensor_tensor(out=last[:], in0=pair[:, 0, half, :], in1=pair[:, 1, half, :], op=ALU.add)
                    nc.sync.dma_start(out=dst[P * (2 + half) : P * (3 + half), dst_col : dst_col + N_TILE], in_=last[:])

        transpose_half(0)
        idle_matmul()
        transpose_half(1)
        idle_matmul()
        transpose_half(2)
        idle_matmul()
        transpose_half(3)
        idle_matmul()
        quantise_half(0)
        fractions_for_re()
        quantise_half(1)
        fractions_for_im()
        make_tables(0, 1)
        make_tables(1, TOKEN_TILES)
        quantise_half(2)
        quantise_half(3)
        acc0 = multiply(0, 0)
        for i in range(4, 8):
            transpose_half(i)
        pair = new_pair()
        finish(0, 0, acc0, pair)
        for i in range(4, 8):
            quantise_half(i)
        acc1 = multiply(0, 1)
        acc2 = multiply(0, 2)
        finish(0, 1, acc1, pair)
        load_words(w_q[2], wq_words[:, :, 2048:3072])
        pending = (0, 2, acc2)
        order = [(0, 3)] + [(b, t) for b in range(1, LAST_ROPE_BLOCK) for t in range(TOKEN_TILES)]
        order.extend([(4, 0), (4, 1), (5, 0), (4, 2), (4, 3), (5, 1), (5, 2), (5, 3)])
        for b, t in order:
            acc = multiply(b, t)
            if t == TOKEN_TILES - 1 and b + PLANES < len(blocks):
                load_scales(planes[b % PLANES], scale_rows[b + PLANES])
                if b == 0:
                    load_words(w_q[3], wq_words[:, :, 3072:4096])
                if b == 1:
                    load_words(w_v, wv_words)
            if pending[1] % 2 == 0 and blocks[pending[0]][3]:
                pair = new_pair()
            finish(pending[0], pending[1], pending[2], pair)
            pending = (b, t, acc)
        finish(pending[0], pending[1], pending[2], pair)
